import numpy as np
import ml_dtypes


def mxq(x, axis, fmt="e4m3"):
    dtype, down = {"e4m3": (ml_dtypes.float8_e4m3fn, 7), "e5m2": (ml_dtypes.float8_e5m2, 14)}[fmt]
    v = np.moveaxis(np.asarray(x, np.float32).astype(ml_dtypes.bfloat16).astype(np.float64), axis, -1)
    blocks = v.reshape(v.shape[:-1] + (-1, 32))
    amax = np.abs(blocks).max(-1, keepdims=True)
    byte = np.maximum(np.where(amax > 0, np.frexp(amax)[1] - 1 + 127, 0) - down, 1)
    scale = np.exp2(byte - 127.0)
    codes = (blocks / scale).astype(np.float32).astype(dtype).astype(np.float64)
    return np.moveaxis((codes * scale).reshape(v.shape), -1, axis)


WIDE = False


def mx_kscale(k):
    if not WIDE:
        return np.ones(k)
    levels = np.array([10, -10, 5, -5, 0])
    a = np.random.permutation(np.resize(levels, k // 512 * 4)).reshape(k // 512, 4)
    idx = np.arange(k)
    return np.exp2(a[idx // 512, idx % 128 // 32])


BF16 = ml_dtypes.bfloat16


def bf(x):
    return np.asarray(x, np.float32).astype(BF16)


def f64(x):
    return np.asarray(x).astype(np.float64)


B, T, DM, DH, L = 4, 512, 1024, 1024, 512


def setup_inputs():
    s, u = mx_kscale(DM), mx_kscale(DM)
    return {"k": bf(np.random.standard_normal((B, T, DM)) * s),
            "v": bf(np.random.standard_normal((B, T, DM)) * u),
            "Wk": bf(np.random.standard_normal((DH, DM)) / np.sqrt(DM) / s),
            "Wv": bf(np.random.standard_normal((DH, DM)) * 3.0 / np.sqrt(DM) / u)}


def reference(k, v, Wk, Wv):
    K = mxq(f64(k), 2, "e4m3") @ mxq(f64(Wk), 1, "e4m3").T
    V = mxq(f64(v), 2, "e4m3") @ mxq(f64(Wv), 1, "e4m3").T
    max_key = K.max(axis=0, keepdims=True)
    exp_key = np.exp(K - max_key)
    return exp_key * V, exp_key

@@ -1,0 +1,219 @@
+from contextlib import ExitStack
+
+import concourse.mybir as mybir
+from concourse.masks import make_identity
+
+F32 = mybir.dt.float32
+BF16 = mybir.dt.bfloat16
+U32 = mybir.dt.uint32
+U8 = mybir.dt.uint8
+FP8X4 = mybir.dt.float8_e4m3fn_x4
+ALU = mybir.AluOpType
+ACT = mybir.ActivationFunctionType
+
+P = 128
+B, T, DM, DH = 4, 512, 1024, 1024
+PACK = 4
+K_PASS = P * PACK
+PASSES = DM // K_PASS
+PAIRS = DM // 2
+SLOTS = PAIRS // P
+BLOCKS = 4
+CHUNK = BLOCKS * P
+N = 512
+HALVES = DH // N
+TOKEN_TILES = T // P
+GROUPS = TOKEN_TILES * HALVES
+LAG = 1
+STEPS = GROUPS + LAG
+K_SIDE = 0
+V_SIDE = 1
+
+FLOPS = 2 * 2 * B * T * DM * DH
+
+
+def chunks_first_used_in(step):
+    found = []
+    for side, group in ((K_SIDE, step), (V_SIDE, step - LAG)):
+        if 0 <= group < GROUPS:
+            token_tile, half = divmod(group, HALVES)
+            if token_tile == 0:
+                found.append((side, "weights", half))
+            if half == 0:
+                found.append((side, "tokens", token_tile))
+    return found
+
+
+def tile_aftfull_pa_kernel(tc, k, v, Wk, Wv, out_0, out_1):
+    nc = tc.nc
+    tokens = (k, v)
+    weights = (Wk, Wv)
+
+    with ExitStack() as stack:
+        const_pool = stack.enter_context(tc.tile_pool(name="const", bufs=1))
+        raw_pool = stack.enter_context(tc.tile_pool(name="raw", bufs=20))
+        grouped_pool = stack.enter_context(tc.tile_pool(name="grouped", bufs=2))
+        mx_pool = stack.enter_context(tc.tile_pool(name="mx", bufs=1))
+        work_pool = stack.enter_context(tc.tile_pool(name="work", bufs=2))
+        out_pool = stack.enter_context(tc.tile_pool(name="outs", bufs=2))
+        turn_psum = stack.enter_context(tc.psum_pool(name="turn", bufs=2))
+        acc_psum = stack.enter_context(tc.psum_pool(name="acc", bufs=6))
+
+        identity = const_pool.tile([P, P], F32, name="identity")
+        make_identity(nc, identity[:])
+
+        stack.enter_context(tc.manual_schedule())
+
+        warm = const_pool.tile([P, 1], F32, name="warm")
+        nc.vector.memset(warm[:], 0.0)
+        nc.scalar.activation(out=warm[:], in_=warm[:], func=ACT.Exp)
+
+        raw = {}
+        grouped = {}
+        codes = {}
+        scales = {}
+
+        def load(chunk):
+            side, kind, index = chunk
+            for block in range(BLOCKS):
+                if kind == "weights":
+                    first = index * CHUNK + block * P
+                    rows = weights[side][first : first + P, :]
+                else:
+                    rows = tokens[side][block, index * P : (index + 1) * P, :]
+                raw[(chunk, block)] = raw_pool.tile([P, DM], BF16, name="raw", tag="raw")
+                nc.sync.dma_start(out=raw[(chunk, block)][:], in_=rows)
+
+        def turn(chunk, block):
+            if block == 0:
+                grouped[chunk] = grouped_pool.tile(
+                    [P, PASSES * CHUNK * PACK], BF16, name="grouped", tag="grouped", align_bytes=64
+                )
+            words = raw[(chunk, block)][:].bitcast(F32)
+            bank = turn_psum.tile([P, SLOTS, P], F32, name="turned", tag="turned")
+            for q in range(SLOTS):
+                nc.tensor.transpose(bank[:, q, :], words[:, q * P : (q + 1) * P], identity[:])
+            pairs = grouped[chunk][:].bitcast(F32).rearrange("p (g r u) -> p g r u", g=PASSES, u=2)
+            nc.scalar.copy(
+                out=pairs[:, :, block * P : (block + 1) * P, :],
+                in_=bank[:].rearrange("p (g u) r -> p g r u", u=2),
+            )
+
+        def quantise(chunk):
+            name = "%d_%s_%d" % chunk
+            codes[chunk] = mx_pool.tile([P, PASSES, CHUNK], U32, name="codes_" + name, align_bytes=64)
+            scales[chunk] = mx_pool.tile([P, PASSES, CHUNK], U8, name="scales_" + name, align_bytes=64)
+            width = CHUNK * PACK
+            for g in range(PASSES):
+                nc.vector.quantize_mx(
+                    out=codes[chunk][:, g, :].bitcast(FP8X4),
+                    scales=scales[chunk][:, g, :],
+                    in_=grouped[chunk][:, g * width : (g + 1) * width],
+                )
+
+        def product(side, group, b):
+            token_tile, half = divmod(group, HALVES)
+            x = (side, "tokens", token_tile)
+            w = (side, "weights", half)
+            rows = slice(b * P, (b + 1) * P)
+            acc = acc_psum.tile([P, N], F32, name="acc", tag="acc")
+            for g in range(PASSES):
+                nc.tensor.matmul_mx(
+                    out=acc[:],
+                    lhsT=codes[x][:, g, rows].bitcast(FP8X4),
+                    lhsT_scale=scales[x][:, g, rows],
+                    rhs=codes[w][:, g, :].bitcast(FP8X4),
+                    rhs_scale=scales[w][:, g, :],
+                    start=(g == 0),
+                    stop=(g == PASSES - 1),
+                )
+            return acc
+
+        for step in range(STEPS):
+            for chunk in chunks_first_used_in(step):
+                load(chunk)
+
+        for chunk in chunks_first_used_in(0):
+            for block in range(BLOCKS):
+                turn(chunk, block)
+            quantise(chunk)
+
+        e_tiles = {}
+        ev_tiles = {}
+
+        for step in range(STEPS):
+            has_k = step < GROUPS
+            has_v = step >= LAG
+            k_tile, k_half = divmod(step, HALVES)
+            v_tile, v_half = divmod(step - LAG, HALVES)
+            k_cols = slice(k_half * N, (k_half + 1) * N)
+            v_cols = slice(v_half * N, (v_half + 1) * N)
+            next_chunks = chunks_first_used_in(step + 1)
+            next_blocks = [(chunk, block) for chunk in next_chunks for block in range(BLOCKS)]
+            middle = len(next_blocks) // 2
+
+            if has_k:
+                big_k = [product(K_SIDE, step, b) for b in range(B)]
+                k_copy = {}
+                for b in (0, 2):
+                    k_copy[b] = work_pool.tile([P, N], F32, name="k_copy%d" % b)
+                    nc.scalar.copy(out=k_copy[b][:], in_=big_k[b][:])
+            for chunk, block in next_blocks[:middle]:
+                turn(chunk, block)
+            if has_v:
+                big_v = [product(V_SIDE, step - LAG, b) for b in (0, 1)]
+            for chunk, block in next_blocks[middle:]:
+                turn(chunk, block)
+            if has_v:
+                big_v.extend([product(V_SIDE, step - LAG, b) for b in (2, 3)])
+
+            def multiply(b):
+                if v_half == 0:
+                    ev_tiles[(v_tile, b)] = out_pool.tile([P, DH], F32, name="ev%d" % b)
+                nc.vector.tensor_tensor(
+                    out=ev_tiles[(v_tile, b)][:, v_cols],
+                    in0=big_v[b][:],
+                    in1=e_tiles[(v_tile, b)][:, v_cols],
+                    op=ALU.mult,
+                )
+
+            if has_k:
+                max_01 = work_pool.tile([P, N], F32, name="max_01")
+                max_23 = work_pool.tile([P, N], F32, name="max_23")
+                max_all = work_pool.tile([P, N], F32, name="max_all")
+                nc.vector.tensor_tensor(out=max_01[:], in0=big_k[1][:], in1=k_copy[0][:], op=ALU.max)
+                nc.vector.tensor_tensor(out=max_23[:], in0=big_k[3][:], in1=k_copy[2][:], op=ALU.max)
+            if has_v:
+                multiply(0)
+            if has_k:
+                nc.vector.tensor_tensor(out=max_all[:], in0=max_01[:], in1=max_23[:], op=ALU.max)
+            if has_v:
+                multiply(1)
+            if has_k:
+                if k_half == 0:
+                    for b in range(B):
+                        e_tiles[(k_tile, b)] = out_pool.tile([P, DH], F32, name="e%d" % b)
+                for b in (1, 3):
+                    nc.vector.tensor_tensor(
+                        out=e_tiles[(k_tile, b)][:, k_cols], in0=big_k[b][:], in1=max_all[:], op=ALU.subtract
+                    )
+                for b in (0, 2):
+                    nc.gpsimd.tensor_tensor(
+                        out=e_tiles[(k_tile, b)][:, k_cols], in0=k_copy[b][:], in1=max_all[:], op=ALU.subtract
+                    )
+            if has_v:
+                multiply(2)
+                multiply(3)
+            if has_k:
+                for b in (1, 3, 0, 2):
+                    part = e_tiles[(k_tile, b)][:, k_cols]
+                    nc.scalar.activation(out=part, in_=part, func=ACT.Exp)
+            for chunk in next_chunks:
+                quantise(chunk)
+
+            if has_k and k_half == HALVES - 1:
+                for b in (1, 3, 0, 2):
+                    nc.sync.dma_start(out=out_1[b, k_tile * P : (k_tile + 1) * P, :], in_=e_tiles[(k_tile, b)][:])
+            if has_v and v_half == HALVES - 1:
+                for b in range(B):
+                    nc.sync.dma_start(out=out_0[b, v_tile * P : (v_tile + 1) * P, :], in_=ev_tiles[(v_tile, b)][:])

@@ -24,23 +24,25 @@ N = 512
 HALVES = DH // N
 TOKEN_TILES = T // P
 GROUPS = TOKEN_TILES * HALVES
-LAG = 1
-STEPS = GROUPS + LAG
 K_SIDE = 0
 V_SIDE = 1
+
+BANKS = {"k0_v1": 1, "k2_v3": 1, "k1": 1, "k3": 1, "turn_v0": 2, "turn_v2": 2}
+K_BANK = {0: "k0_v1", 1: "k1", 2: "k2_v3", 3: "k3"}
+V_BANK = {0: "turn_v0", 1: "k0_v1", 2: "turn_v2", 3: "k2_v3"}
+TURN_BANK = ("turn_v0", "turn_v2")
 
 FLOPS = 2 * 2 * B * T * DM * DH
 
 
-def chunks_first_used_in(step):
+def chunks_first_used_by(side, group):
     found = []
-    for side, group in ((K_SIDE, step), (V_SIDE, step - LAG)):
-        if 0 <= group < GROUPS:
-            token_tile, half = divmod(group, HALVES)
-            if token_tile == 0:
-                found.append((side, "weights", half))
-            if half == 0:
-                found.append((side, "tokens", token_tile))
+    if 0 <= group < GROUPS:
+        token_tile, half = divmod(group, HALVES)
+        if token_tile == 0:
+            found.append((side, "weights", half))
+        if half == 0:
+            found.append((side, "tokens", token_tile))
     return found
 
 
@@ -49,15 +51,22 @@ def tile_aftfull_pa_kernel(tc, k, v, Wk, Wv, out_0, out_1):
     tokens = (k, v)
     weights = (Wk, Wv)
 
+    first_chunks = (
+        chunks_first_used_by(K_SIDE, 0) + chunks_first_used_by(K_SIDE, 1) + chunks_first_used_by(V_SIDE, 0)
+    )
+    chunks_of_period = [
+        chunks_first_used_by(K_SIDE, period + 2) + chunks_first_used_by(V_SIDE, period + 1)
+        for period in range(GROUPS + 1)
+    ]
+
     with ExitStack() as stack:
         const_pool = stack.enter_context(tc.tile_pool(name="const", bufs=1))
         raw_pool = stack.enter_context(tc.tile_pool(name="raw", bufs=20))
         grouped_pool = stack.enter_context(tc.tile_pool(name="grouped", bufs=2))
         mx_pool = stack.enter_context(tc.tile_pool(name="mx", bufs=1))
         work_pool = stack.enter_context(tc.tile_pool(name="work", bufs=2))
-        out_pool = stack.enter_context(tc.tile_pool(name="outs", bufs=2))
-        turn_psum = stack.enter_context(tc.psum_pool(name="turn", bufs=2))
-        acc_psum = stack.enter_context(tc.psum_pool(name="acc", bufs=6))
+        out_pool = stack.enter_context(tc.tile_pool(name="outs", bufs=3))
+        psum = stack.enter_context(tc.psum_pool(name="psum", bufs=1))
 
         identity = const_pool.tile([P, P], F32, name="identity")
         make_identity(nc, identity[:])
@@ -72,6 +81,10 @@ def tile_aftfull_pa_kernel(tc, k, v, Wk, Wv, out_0, out_1):
         grouped = {}
         codes = {}
         scales = {}
+        e_tiles = {}
+
+        def bank(name):
+            return psum.tile([P, N], F32, name=name, tag=name, bufs=BANKS[name])
 
         def load(chunk):
             side, kind, index = chunk
@@ -90,13 +103,13 @@ def tile_aftfull_pa_kernel(tc, k, v, Wk, Wv, out_0, out_1):
                     [P, PASSES * CHUNK * PACK], BF16, name="grouped", tag="grouped", align_bytes=64
                 )
             words = raw[(chunk, block)][:].bitcast(F32)
-            bank = turn_psum.tile([P, SLOTS, P], F32, name="turned", tag="turned")
+            turned = bank(TURN_BANK[block % 2])
             for q in range(SLOTS):
-                nc.tensor.transpose(bank[:, q, :], words[:, q * P : (q + 1) * P], identity[:])
+                nc.tensor.transpose(turned[:, q * P : (q + 1) * P], words[:, q * P : (q + 1) * P], identity[:])
             pairs = grouped[chunk][:].bitcast(F32).rearrange("p (g r u) -> p g r u", g=PASSES, u=2)
             nc.scalar.copy(
                 out=pairs[:, :, block * P : (block + 1) * P, :],
-                in_=bank[:].rearrange("p (g u) r -> p g r u", u=2),
+                in_=turned[:].rearrange("p (g u r) -> p g r u", g=PASSES, u=2),
             )
 
         def quantise(chunk):
@@ -116,7 +129,7 @@ def tile_aftfull_pa_kernel(tc, k, v, Wk, Wv, out_0, out_1):
             x = (side, "tokens", token_tile)
             w = (side, "weights", half)
             rows = slice(b * P, (b + 1) * P)
-            acc = acc_psum.tile([P, N], F32, name="acc", tag="acc")
+            acc = bank(K_BANK[b] if side == K_SIDE else V_BANK[b])
             for g in range(PASSES):
                 nc.tensor.matmul_mx(
                     out=acc[:],
@@ -129,53 +142,56 @@ def tile_aftfull_pa_kernel(tc, k, v, Wk, Wv, out_0, out_1):
                 )
             return acc
 
-        for step in range(STEPS):
-            for chunk in chunks_first_used_in(step):
+        def k_products(group):
+            big_k = {}
+            k_copy = {}
+            for b in (0, 2, 1, 3):
+                big_k[b] = product(K_SIDE, group, b)
+            for b in (0, 2):
+                k_copy[b] = work_pool.tile([P, N], F32, name="k_copy%d" % b)
+                nc.scalar.copy(out=k_copy[b][:], in_=big_k[b][:])
+            return big_k, k_copy
+
+        def place(group, b):
+            token_tile, half = divmod(group, HALVES)
+            return (b, slice(token_tile * P, (token_tile + 1) * P), slice(half * N, (half + 1) * N))
+
+        def exp_and_store(group, b):
+            e = e_tiles[(group, b)]
+            nc.scalar.activation(out=e[:], in_=e[:], func=ACT.Exp)
+            nc.sync.dma_start(out=out_1[place(group, b)], in_=e[:])
+
+        def multiply_and_store(group, b, big_v):
+            ev = out_pool.tile([P, N], F32, name="ev%d" % b)
+            nc.vector.tensor_tensor(out=ev[:], in0=big_v[:], in1=e_tiles[(group, b)][:], op=ALU.mult)
+            nc.sync.dma_start(out=out_0[place(group, b)], in_=ev[:])
+
+        for chunk in first_chunks:
+            load(chunk)
+        for chunks in chunks_of_period:
+            for chunk in chunks:
                 load(chunk)
 
-        for chunk in chunks_first_used_in(0):
+        for i, chunk in enumerate(first_chunks):
             for block in range(BLOCKS):
                 turn(chunk, block)
-            quantise(chunk)
+            if i > 0:
+                quantise(first_chunks[i - 1])
+        quantise(first_chunks[-1])
+        big_k, k_copy = k_products(0)
 
-        e_tiles = {}
-        ev_tiles = {}
+        for period in range(GROUPS + 1):
+            group = period
+            v_group = period - 1
+            has_k = group < GROUPS
+            has_v = v_group >= 0
+            blocks = [(chunk, block) for chunk in chunks_of_period[period] for block in range(BLOCKS)]
+            middle = len(blocks) // 2
+            big_v = {}
 
-        for step in range(STEPS):
-            has_k = step < GROUPS
-            has_v = step >= LAG
-            k_tile, k_half = divmod(step, HALVES)
-            v_tile, v_half = divmod(step - LAG, HALVES)
-            k_cols = slice(k_half * N, (k_half + 1) * N)
-            v_cols = slice(v_half * N, (v_half + 1) * N)
-            next_chunks = chunks_first_used_in(step + 1)
-            next_blocks = [(chunk, block) for chunk in next_chunks for block in range(BLOCKS)]
-            middle = len(next_blocks) // 2
-
-            if has_k:
-                big_k = [product(K_SIDE, step, b) for b in range(B)]
-                k_copy = {}
-                for b in (0, 2):
-                    k_copy[b] = work_pool.tile([P, N], F32, name="k_copy%d" % b)
-                    nc.scalar.copy(out=k_copy[b][:], in_=big_k[b][:])
-            for chunk, block in next_blocks[:middle]:
-                turn(chunk, block)
             if has_v:
-                big_v = [product(V_SIDE, step - LAG, b) for b in (0, 1)]
-            for chunk, block in next_blocks[middle:]:
-                turn(chunk, block)
-            if has_v:
-                big_v.extend([product(V_SIDE, step - LAG, b) for b in (2, 3)])
-
-            def multiply(b):
-                if v_half == 0:
-                    ev_tiles[(v_tile, b)] = out_pool.tile([P, DH], F32, name="ev%d" % b)
-                nc.vector.tensor_tensor(
-                    out=ev_tiles[(v_tile, b)][:, v_cols],
-                    in0=big_v[b][:],
-                    in1=e_tiles[(v_tile, b)][:, v_cols],
-                    op=ALU.mult,
-                )
+                for b in (1, 3):
+                    big_v[b] = product(V_SIDE, v_group, b)
 
             if has_k:
                 max_01 = work_pool.tile([P, N], F32, name="max_01")
@@ -184,36 +200,36 @@ def tile_aftfull_pa_kernel(tc, k, v, Wk, Wv, out_0, out_1):
                 nc.vector.tensor_tensor(out=max_01[:], in0=big_k[1][:], in1=k_copy[0][:], op=ALU.max)
                 nc.vector.tensor_tensor(out=max_23[:], in0=big_k[3][:], in1=k_copy[2][:], op=ALU.max)
             if has_v:
-                multiply(0)
+                multiply_and_store(v_group, 1, big_v[1])
             if has_k:
                 nc.vector.tensor_tensor(out=max_all[:], in0=max_01[:], in1=max_23[:], op=ALU.max)
             if has_v:
-                multiply(1)
+                multiply_and_store(v_group, 3, big_v[3])
             if has_k:
-                if k_half == 0:
-                    for b in range(B):
-                        e_tiles[(k_tile, b)] = out_pool.tile([P, DH], F32, name="e%d" % b)
-                for b in (1, 3):
-                    nc.vector.tensor_tensor(
-                        out=e_tiles[(k_tile, b)][:, k_cols], in0=big_k[b][:], in1=max_all[:], op=ALU.subtract
-                    )
-                for b in (0, 2):
-                    nc.gpsimd.tensor_tensor(
-                        out=e_tiles[(k_tile, b)][:, k_cols], in0=k_copy[b][:], in1=max_all[:], op=ALU.subtract
-                    )
-            if has_v:
-                multiply(2)
-                multiply(3)
-            if has_k:
-                for b in (1, 3, 0, 2):
-                    part = e_tiles[(k_tile, b)][:, k_cols]
-                    nc.scalar.activation(out=part, in_=part, func=ACT.Exp)
-            for chunk in next_chunks:
-                quantise(chunk)
-
-            if has_k and k_half == HALVES - 1:
-                for b in (1, 3, 0, 2):
-                    nc.sync.dma_start(out=out_1[b, k_tile * P : (k_tile + 1) * P, :], in_=e_tiles[(k_tile, b)][:])
-            if has_v and v_half == HALVES - 1:
                 for b in range(B):
-                    nc.sync.dma_start(out=out_0[b, v_tile * P : (v_tile + 1) * P, :], in_=ev_tiles[(v_tile, b)][:])
+                    e_tiles[(group, b)] = out_pool.tile([P, N], F32, name="e%d" % b)
+                for b in (1, 3):
+                    nc.vector.tensor_tensor(out=e_tiles[(group, b)][:], in0=big_k[b][:], in1=max_all[:], op=ALU.subtract)
+                for b in (0, 2):
+                    nc.gpsimd.tensor_tensor(out=e_tiles[(group, b)][:], in0=k_copy[b][:], in1=max_all[:], op=ALU.subtract)
+
+            for chunk, block in blocks[:middle]:
+                turn(chunk, block)
+            if has_v:
+                for b in (0, 2):
+                    exp_and_store(v_group, b)
+                for b in (0, 2):
+                    big_v[b] = product(V_SIDE, v_group, b)
+                for b in (0, 2):
+                    multiply_and_store(v_group, b, big_v[b])
+            for chunk, block in blocks[middle:]:
+                turn(chunk, block)
+            for chunk in chunks_of_period[period]:
+                quantise(chunk)
+            if group + 1 < GROUPS:
+                big_k_next, k_copy_next = k_products(group + 1)
+            if has_k:
+                for b in (1, 3):
+                    exp_and_store(group, b)
+            if group + 1 < GROUPS:
+                big_k, k_copy = big_k_next, k_copy_next

@@ -65,7 +65,8 @@ def tile_aftfull_pa_kernel(tc, k, v, Wk, Wv, out_0, out_1):
         grouped_pool = stack.enter_context(tc.tile_pool(name="grouped", bufs=2))
         mx_pool = stack.enter_context(tc.tile_pool(name="mx", bufs=1))
         work_pool = stack.enter_context(tc.tile_pool(name="work", bufs=2))
-        out_pool = stack.enter_context(tc.tile_pool(name="outs", bufs=3))
+        e_pool = stack.enter_context(tc.tile_pool(name="e", bufs=3))
+        ev_pool = stack.enter_context(tc.tile_pool(name="ev", bufs=1))
         psum = stack.enter_context(tc.psum_pool(name="psum", bufs=1))
 
         identity = const_pool.tile([P, P], F32, name="identity")
@@ -82,6 +83,7 @@ def tile_aftfull_pa_kernel(tc, k, v, Wk, Wv, out_0, out_1):
         codes = {}
         scales = {}
         e_tiles = {}
+        ev_tiles = {}
 
         def bank(name):
             return psum.tile([P, N], F32, name=name, tag=name, bufs=BANKS[name])
@@ -116,13 +118,11 @@ def tile_aftfull_pa_kernel(tc, k, v, Wk, Wv, out_0, out_1):
             name = "%d_%s_%d" % chunk
             codes[chunk] = mx_pool.tile([P, PASSES, CHUNK], U32, name="codes_" + name, align_bytes=64)
             scales[chunk] = mx_pool.tile([P, PASSES, CHUNK], U8, name="scales_" + name, align_bytes=64)
-            width = CHUNK * PACK
-            for g in range(PASSES):
-                nc.vector.quantize_mx(
-                    out=codes[chunk][:, g, :].bitcast(FP8X4),
-                    scales=scales[chunk][:, g, :],
-                    in_=grouped[chunk][:, g * width : (g + 1) * width],
-                )
+            nc.vector.quantize_mx(
+                out=codes[chunk][:].rearrange("p g r -> p (g r)").bitcast(FP8X4),
+                scales=scales[chunk][:].rearrange("p g r -> p (g r)"),
+                in_=grouped[chunk][:],
+            )
 
         def product(side, group, b):
             token_tile, half = divmod(group, HALVES)
@@ -144,27 +144,36 @@ def tile_aftfull_pa_kernel(tc, k, v, Wk, Wv, out_0, out_1):
 
         def k_products(group):
             big_k = {}
-            k_copy = {}
             for b in (0, 2, 1, 3):
                 big_k[b] = product(K_SIDE, group, b)
+            k_copy = work_pool.tile([P, 2, N], F32, name="k_copy")
             for b in (0, 2):
-                k_copy[b] = work_pool.tile([P, N], F32, name="k_copy%d" % b)
-                nc.scalar.copy(out=k_copy[b][:], in_=big_k[b][:])
+                nc.scalar.copy(out=k_copy[:, b // 2, :], in_=big_k[b][:])
             return big_k, k_copy
 
-        def place(group, b):
+        def pair_in(out, group, parity):
             token_tile, half = divmod(group, HALVES)
-            return (b, slice(token_tile * P, (token_tile + 1) * P), slice(half * N, (half + 1) * N))
+            part = out[parity:B:2, token_tile * P : (token_tile + 1) * P, half * N : (half + 1) * N]
+            return part.rearrange("b p c -> p b c")
 
-        def exp_and_store(group, b):
-            e = e_tiles[(group, b)]
-            nc.scalar.activation(out=e[:], in_=e[:], func=ACT.Exp)
-            nc.sync.dma_start(out=out_1[place(group, b)], in_=e[:])
+        def exp_and_store(group, parity):
+            e = e_tiles[(group, parity)]
+            flat = e[:].rearrange("p b c -> p (b c)")
+            nc.scalar.activation(out=flat, in_=flat, func=ACT.Exp)
+            nc.sync.dma_start(out=pair_in(out_1, group, parity), in_=e[:])
 
-        def multiply_and_store(group, b, big_v):
-            ev = out_pool.tile([P, N], F32, name="ev%d" % b)
-            nc.vector.tensor_tensor(out=ev[:], in0=big_v[:], in1=e_tiles[(group, b)][:], op=ALU.mult)
-            nc.sync.dma_start(out=out_0[place(group, b)], in_=ev[:])
+        def multiply(group, b, big_v):
+            parity = b % 2
+            if b == parity:
+                ev_tiles[(group, parity)] = ev_pool.tile([P, 2, N], F32, name="ev_%d_%d" % (group, parity))
+            nc.vector.tensor_tensor(
+                out=ev_tiles[(group, parity)][:, b // 2, :],
+                in0=big_v[:],
+                in1=e_tiles[(group, parity)][:, b // 2, :],
+                op=ALU.mult,
+            )
+            if b == parity + 2:
+                nc.sync.dma_start(out=pair_in(out_0, group, parity), in_=ev_tiles[(group, parity)][:])
 
         for chunk in first_chunks:
             load(chunk)
@@ -197,31 +206,34 @@ def tile_aftfull_pa_kernel(tc, k, v, Wk, Wv, out_0, out_1):
                 max_01 = work_pool.tile([P, N], F32, name="max_01")
                 max_23 = work_pool.tile([P, N], F32, name="max_23")
                 max_all = work_pool.tile([P, N], F32, name="max_all")
-                nc.vector.tensor_tensor(out=max_01[:], in0=big_k[1][:], in1=k_copy[0][:], op=ALU.max)
-                nc.vector.tensor_tensor(out=max_23[:], in0=big_k[3][:], in1=k_copy[2][:], op=ALU.max)
+                nc.vector.tensor_tensor(out=max_01[:], in0=big_k[1][:], in1=k_copy[:, 0, :], op=ALU.max)
+                nc.vector.tensor_tensor(out=max_23[:], in0=big_k[3][:], in1=k_copy[:, 1, :], op=ALU.max)
             if has_v:
-                multiply_and_store(v_group, 1, big_v[1])
+                multiply(v_group, 1, big_v[1])
             if has_k:
                 nc.vector.tensor_tensor(out=max_all[:], in0=max_01[:], in1=max_23[:], op=ALU.max)
             if has_v:
-                multiply_and_store(v_group, 3, big_v[3])
+                multiply(v_group, 3, big_v[3])
             if has_k:
-                for b in range(B):
-                    e_tiles[(group, b)] = out_pool.tile([P, N], F32, name="e%d" % b)
+                for parity in (0, 1):
+                    e_tiles[(group, parity)] = e_pool.tile([P, 2, N], F32, name="e_%d" % parity)
                 for b in (1, 3):
-                    nc.vector.tensor_tensor(out=e_tiles[(group, b)][:], in0=big_k[b][:], in1=max_all[:], op=ALU.subtract)
+                    nc.vector.tensor_tensor(
+                        out=e_tiles[(group, 1)][:, b // 2, :], in0=big_k[b][:], in1=max_all[:], op=ALU.subtract
+                    )
                 for b in (0, 2):
-                    nc.gpsimd.tensor_tensor(out=e_tiles[(group, b)][:], in0=k_copy[b][:], in1=max_all[:], op=ALU.subtract)
+                    nc.gpsimd.tensor_tensor(
+                        out=e_tiles[(group, 0)][:, b // 2, :], in0=k_copy[:, b // 2, :], in1=max_all[:], op=ALU.subtract
+                    )
 
             for chunk, block in blocks[:middle]:
                 turn(chunk, block)
             if has_v:
-                for b in (0, 2):
-                    exp_and_store(v_group, b)
+                exp_and_store(v_group, 0)
                 for b in (0, 2):
                     big_v[b] = product(V_SIDE, v_group, b)
                 for b in (0, 2):
-                    multiply_and_store(v_group, b, big_v[b])
+                    multiply(v_group, b, big_v[b])
             for chunk, block in blocks[middle:]:
                 turn(chunk, block)
             for chunk in chunks_of_period[period]:
@@ -229,7 +241,6 @@ def tile_aftfull_pa_kernel(tc, k, v, Wk, Wv, out_0, out_1):
             if group + 1 < GROUPS:
                 big_k_next, k_copy_next = k_products(group + 1)
             if has_k:
-                for b in (1, 3):
-                    exp_and_store(group, b)
+                exp_and_store(group, 1)
             if group + 1 < GROUPS:
                 big_k, k_copy = big_k_next, k_copy_next

from contextlib import ExitStack

import concourse.mybir as mybir
from concourse.masks import make_identity

F32 = mybir.dt.float32
BF16 = mybir.dt.bfloat16
U32 = mybir.dt.uint32
U8 = mybir.dt.uint8
FP8X4 = mybir.dt.float8_e4m3fn_x4
ALU = mybir.AluOpType
ACT = mybir.ActivationFunctionType

P = 128
B, T, DM, DH = 4, 512, 1024, 1024
PACK = 4
K_PASS = P * PACK
PASSES = DM // K_PASS
PAIRS = DM // 2
SLOTS = PAIRS // P
BLOCKS = 4
CHUNK = BLOCKS * P
N = 512
HALVES = DH // N
TOKEN_TILES = T // P
GROUPS = TOKEN_TILES * HALVES
K_SIDE = 0
V_SIDE = 1

BANKS = {"k0_v1": 1, "k2_v3": 1, "k1": 1, "k3": 1, "turn_v0": 2, "turn_v2": 2}
K_BANK = {0: "k0_v1", 1: "k1", 2: "k2_v3", 3: "k3"}
V_BANK = {0: "turn_v0", 1: "k0_v1", 2: "turn_v2", 3: "k2_v3"}
TURN_BANK = ("turn_v0", "turn_v2")

FLOPS = 2 * 2 * B * T * DM * DH


def chunks_first_used_by(side, group):
    found = []
    if 0 <= group < GROUPS:
        token_tile, half = divmod(group, HALVES)
        if token_tile == 0:
            found.append((side, "weights", half))
        if half == 0:
            found.append((side, "tokens", token_tile))
    return found


def tile_aftfull_pa_kernel(tc, k, v, Wk, Wv, out_0, out_1):
    nc = tc.nc
    tokens = (k, v)
    weights = (Wk, Wv)

    first_chunks = (
        chunks_first_used_by(K_SIDE, 0) + chunks_first_used_by(K_SIDE, 1) + chunks_first_used_by(V_SIDE, 0)
    )
    chunks_of_period = [
        chunks_first_used_by(K_SIDE, period + 2) + chunks_first_used_by(V_SIDE, period + 1)
        for period in range(GROUPS + 1)
    ]

    with ExitStack() as stack:
        const_pool = stack.enter_context(tc.tile_pool(name="const", bufs=1))
        raw_pool = stack.enter_context(tc.tile_pool(name="raw", bufs=20))
        grouped_pool = stack.enter_context(tc.tile_pool(name="grouped", bufs=2))
        mx_pool = stack.enter_context(tc.tile_pool(name="mx", bufs=1))
        work_pool = stack.enter_context(tc.tile_pool(name="work", bufs=2))
        e_pool = stack.enter_context(tc.tile_pool(name="e", bufs=3))
        ev_pool = stack.enter_context(tc.tile_pool(name="ev", bufs=1))
        psum = stack.enter_context(tc.psum_pool(name="psum", bufs=1))

        identity = const_pool.tile([P, P], F32, name="identity")
        make_identity(nc, identity[:])

        stack.enter_context(tc.manual_schedule())

        warm = const_pool.tile([P, 1], F32, name="warm")
        nc.vector.memset(warm[:], 0.0)
        nc.scalar.activation(out=warm[:], in_=warm[:], func=ACT.Exp)

        raw = {}
        grouped = {}
        codes = {}
        scales = {}
        e_tiles = {}
        ev_tiles = {}

        def bank(name):
            return psum.tile([P, N], F32, name=name, tag=name, bufs=BANKS[name])

        def load(chunk):
            side, kind, index = chunk
            for block in range(BLOCKS):
                if kind == "weights":
                    first = index * CHUNK + block * P
                    rows = weights[side][first : first + P, :]
                else:
                    rows = tokens[side][block, index * P : (index + 1) * P, :]
                raw[(chunk, block)] = raw_pool.tile([P, DM], BF16, name="raw", tag="raw")
                nc.sync.dma_start(out=raw[(chunk, block)][:], in_=rows)

        def turn(chunk, block):
            if block == 0:
                grouped[chunk] = grouped_pool.tile(
                    [P, PASSES * CHUNK * PACK], BF16, name="grouped", tag="grouped", align_bytes=64
                )
            words = raw[(chunk, block)][:].bitcast(F32)
            turned = bank(TURN_BANK[block % 2])
            for q in range(SLOTS):
                nc.tensor.transpose(turned[:, q * P : (q + 1) * P], words[:, q * P : (q + 1) * P], identity[:])
            pairs = grouped[chunk][:].bitcast(F32).rearrange("p (g r u) -> p g r u", g=PASSES, u=2)
            nc.scalar.copy(
                out=pairs[:, :, block * P : (block + 1) * P, :],
                in_=turned[:].rearrange("p (g u r) -> p g r u", g=PASSES, u=2),
            )

        def quantise(chunk):
            name = "%d_%s_%d" % chunk
            codes[chunk] = mx_pool.tile([P, PASSES, CHUNK], U32, name="codes_" + name, align_bytes=64)
            scales[chunk] = mx_pool.tile([P, PASSES, CHUNK], U8, name="scales_" + name, align_bytes=64)
            nc.vector.quantize_mx(
                out=codes[chunk][:].rearrange("p g r -> p (g r)").bitcast(FP8X4),
                scales=scales[chunk][:].rearrange("p g r -> p (g r)"),
                in_=grouped[chunk][:],
            )

        def product(side, group, b):
            token_tile, half = divmod(group, HALVES)
            x = (side, "tokens", token_tile)
            w = (side, "weights", half)
            rows = slice(b * P, (b + 1) * P)
            acc = bank(K_BANK[b] if side == K_SIDE else V_BANK[b])
            for g in range(PASSES):
                nc.tensor.matmul_mx(
                    out=acc[:],
                    lhsT=codes[x][:, g, rows].bitcast(FP8X4),
                    lhsT_scale=scales[x][:, g, rows],
                    rhs=codes[w][:, g, :].bitcast(FP8X4),
                    rhs_scale=scales[w][:, g, :],
                    start=(g == 0),
                    stop=(g == PASSES - 1),
                )
            return acc

        def k_products(group):
            big_k = {}
            for b in (0, 2, 1, 3):
                big_k[b] = product(K_SIDE, group, b)
            k_copy = work_pool.tile([P, 2, N], F32, name="k_copy")
            for b in (0, 2):
                nc.scalar.copy(out=k_copy[:, b // 2, :], in_=big_k[b][:])
            return big_k, k_copy

        def pair_in(out, group, parity):
            token_tile, half = divmod(group, HALVES)
            part = out[parity:B:2, token_tile * P : (token_tile + 1) * P, half * N : (half + 1) * N]
            return part.rearrange("b p c -> p b c")

        def exp_and_store(group, parity):
            e = e_tiles[(group, parity)]
            flat = e[:].rearrange("p b c -> p (b c)")
            nc.scalar.activation(out=flat, in_=flat, func=ACT.Exp)
            nc.sync.dma_start(out=pair_in(out_1, group, parity), in_=e[:])

        def multiply(group, b, big_v):
            parity = b % 2
            if b == parity:
                ev_tiles[(group, parity)] = ev_pool.tile([P, 2, N], F32, name="ev_%d_%d" % (group, parity))
            nc.vector.tensor_tensor(
                out=ev_tiles[(group, parity)][:, b // 2, :],
                in0=big_v[:],
                in1=e_tiles[(group, parity)][:, b // 2, :],
                op=ALU.mult,
            )
            if b == parity + 2:
                nc.sync.dma_start(out=pair_in(out_0, group, parity), in_=ev_tiles[(group, parity)][:])

        for chunk in first_chunks:
            load(chunk)
        for chunks in chunks_of_period:
            for chunk in chunks:
                load(chunk)

        for i, chunk in enumerate(first_chunks):
            for block in range(BLOCKS):
                turn(chunk, block)
            if i > 0:
                quantise(first_chunks[i - 1])
        quantise(first_chunks[-1])
        big_k, k_copy = k_products(0)

        for period in range(GROUPS + 1):
            group = period
            v_group = period - 1
            has_k = group < GROUPS
            has_v = v_group >= 0
            blocks = [(chunk, block) for chunk in chunks_of_period[period] for block in range(BLOCKS)]
            middle = len(blocks) // 2
            big_v = {}

            if has_v:
                for b in (1, 3):
                    big_v[b] = product(V_SIDE, v_group, b)

            if has_k:
                max_01 = work_pool.tile([P, N], F32, name="max_01")
                max_23 = work_pool.tile([P, N], F32, name="max_23")
                max_all = work_pool.tile([P, N], F32, name="max_all")
                nc.vector.tensor_tensor(out=max_01[:], in0=big_k[1][:], in1=k_copy[:, 0, :], op=ALU.max)
                nc.vector.tensor_tensor(out=max_23[:], in0=big_k[3][:], in1=k_copy[:, 1, :], op=ALU.max)
            if has_v:
                multiply(v_group, 1, big_v[1])
            if has_k:
                nc.vector.tensor_tensor(out=max_all[:], in0=max_01[:], in1=max_23[:], op=ALU.max)
            if has_v:
                multiply(v_group, 3, big_v[3])
            if has_k:
                for parity in (0, 1):
                    e_tiles[(group, parity)] = e_pool.tile([P, 2, N], F32, name="e_%d" % parity)
                for b in (1, 3):
                    nc.vector.tensor_tensor(
                        out=e_tiles[(group, 1)][:, b // 2, :], in0=big_k[b][:], in1=max_all[:], op=ALU.subtract
                    )
                for b in (0, 2):
                    nc.gpsimd.tensor_tensor(
                        out=e_tiles[(group, 0)][:, b // 2, :], in0=k_copy[:, b // 2, :], in1=max_all[:], op=ALU.subtract
                    )

            for chunk, block in blocks[:middle]:
                turn(chunk, block)
            if has_v:
                exp_and_store(v_group, 0)
                for b in (0, 2):
                    big_v[b] = product(V_SIDE, v_group, b)
                for b in (0, 2):
                    multiply(v_group, b, big_v[b])
            for chunk, block in blocks[middle:]:
                turn(chunk, block)
            for chunk in chunks_of_period[period]:
                quantise(chunk)
            if group + 1 < GROUPS:
                big_k_next, k_copy_next = k_products(group + 1)
            if has_k:
                exp_and_store(group, 1)
            if group + 1 < GROUPS:
                big_k, k_copy = big_k_next, k_copy_next
